import numpy as np
import ml_dtypes


def mxq(x, axis, fmt="e4m3"):
    dtype, down = {"e4m3": (ml_dtypes.float8_e4m3fn, 7), "e5m2": (ml_dtypes.float8_e5m2, 14)}[fmt]
    v = np.moveaxis(np.asarray(x, np.float32).astype(ml_dtypes.bfloat16).astype(np.float64), axis, -1)
    blocks = v.reshape(v.shape[:-1] + (-1, 32))
    amax = np.abs(blocks).max(-1, keepdims=True)
    byte = np.maximum(np.where(amax > 0, np.frexp(amax)[1] - 1 + 127, 0) - down, 1)
    scale = np.exp2(byte - 127.0)
    codes = (blocks / scale).astype(np.float32).astype(dtype).astype(np.float64)
    return np.moveaxis((codes * scale).reshape(v.shape), -1, axis)


WIDE = False


def mx_kscale(k):
    if not WIDE:
        return np.ones(k)
    levels = np.array([10, -10, 5, -5, 0])
    a = np.random.permutation(np.resize(levels, k // 512 * 4)).reshape(k // 512, 4)
    idx = np.arange(k)
    return np.exp2(a[idx // 512, idx % 128 // 32])


BF16 = ml_dtypes.bfloat16


def bf(x):
    return np.asarray(x, np.float32).astype(BF16)


def f64(x):
    return np.asarray(x).astype(np.float64)


B, T, H, D = 2, 512, 2, 512
A = 1.5 / D ** 0.25


def relative_shift(x):
    b, h, t, tt = x.shape
    x = np.pad(x, [[0, 0], [0, 0], [0, 0], [1, 0]])
    x = x.reshape(b, h, tt + 1, t)[:, :, 1:, :]
    return x.reshape(b, h, t, tt)


def setup_inputs():
    s = mx_kscale(D)
    return {"q": bf(np.random.standard_normal((B, T, H, D)) * A * s),
            "k": bf(np.random.standard_normal((B, T, H, D)) * A / s),
            "r_w_bias": bf(np.random.standard_normal((H, D)) * 0.5 * A * s),
            "r_r_bias": bf(np.random.standard_normal((H, D)) * 0.5 * A * s),
            "rel_pos_emb": bf(np.random.standard_normal((T, H, D)) * A / s)}


def reference(q, k, r_w_bias, r_r_bias, rel_pos_emb):
    qw = (f64(q) + f64(r_w_bias)).transpose(0, 2, 1, 3)
    qr = (f64(q) + f64(r_r_bias)).transpose(0, 2, 1, 3)
    kt = f64(k).transpose(0, 2, 3, 1)
    rt = f64(rel_pos_emb).transpose(1, 2, 0)
    content = mxq(qw, 3, "e4m3") @ mxq(kt, 2, "e4m3")
    rel = mxq(qr, 3, "e4m3") @ mxq(rt, 1, "e4m3")
    return content + relative_shift(rel)

@@ -1,0 +1,182 @@
+from contextlib import ExitStack
+
+import concourse.mybir as mybir
+from concourse.masks import make_identity
+
+F32 = mybir.dt.float32
+BF16 = mybir.dt.bfloat16
+U32 = mybir.dt.uint32
+U8 = mybir.dt.uint8
+FP8X4 = mybir.dt.float8_e4m3fn_x4
+ADD = mybir.AluOpType.add
+
+B, T, H, D = 2, 512, 2, 512
+P = 128
+A = T // P
+PADDED = T + 1
+FLOPS = 2 * 2 * B * H * T * T * D
+
+
+def tile_relativepositionembedding_pa_kernel(tc, q, k, r_w_bias, r_r_bias, rel_pos_emb, out):
+    nc = tc.nc
+    with ExitStack() as ctx:
+
+        const = ctx.enter_context(tc.tile_pool(name="const", bufs=1))
+        inp = ctx.enter_context(tc.tile_pool(name="inp", bufs=1))
+        grp = ctx.enter_context(tc.tile_pool(name="grp", bufs=1))
+        cod = ctx.enter_context(tc.tile_pool(name="cod", bufs=1))
+        big = ctx.enter_context(tc.tile_pool(name="big", bufs=4))
+        psum = ctx.enter_context(tc.psum_pool(name="psum", bufs=4))
+
+        bias_sb = const.tile([P, D], BF16)
+        nc.vector.memset(bias_sb[:], 0.0)
+        nc.sync.dma_start(out=bias_sb[0:2, :], in_=r_w_bias)
+        nc.sync.dma_start(out=bias_sb[2:4, :], in_=r_r_bias)
+        ident = const.tile([P, P], F32)
+        make_identity(nc, ident[:])
+
+        def load(src, name):
+            t = inp.tile([P, A, H, D], BF16, name=name)
+            nc.sync.dma_start(out=t[:], in_=src.rearrange("(p a) h d -> p a h d", a=A))
+            return t
+
+        q_sb = [None, None]
+        k_sb = [None, None]
+        q_sb[0] = load(q[0], "q_sb0")
+        r_sb = load(rel_pos_emb, "r_sb")
+        q_sb[1] = load(q[1], "q_sb1")
+        k_sb[0] = load(k[0], "k_sb0")
+        k_sb[1] = load(k[1], "k_sb1")
+
+        zt = []
+        for i in range(B * H):
+            z = big.tile([P, A, PADDED], F32, name="z%d" % i, tag="big")
+            nc.vector.memset(z[:, :, 0:2], 0.0)
+            zt.append(z)
+
+        bias4 = const.tile([P, 4, 4], BF16)
+        bw = bias_sb[:].bitcast(F32)
+        bbank = psum.tile([P, 2, 256], F32, name="bbank", tag="tp")
+        for u in range(2):
+            nc.tensor.transpose(bbank[:, u, 0:P], bw[:, P * u : P * (u + 1)], ident[:])
+        nc.vector.tensor_copy(out=bias4[:].bitcast(F32), in_=bbank[:, :, 0:4].rearrange("p u r -> p r u"))
+
+        def transposes(x_sb, h, ap, name):
+            xw = x_sb[:].bitcast(F32)
+            bank = psum.tile([P, 2, 256], F32, name=name, tag="tp")
+            for u in range(2):
+                for i in range(2):
+                    nc.tensor.transpose(
+                        bank[:, u, P * i : P * (i + 1)], xw[:, 2 * ap + i, h, P * u : P * (u + 1)], ident[:]
+                    )
+            return bank
+
+        def mx_tiles(name):
+            g = grp.tile([P, H, T, 4], BF16, name=name + "_g", align_bytes=64)
+            c = cod.tile([P, H, T], U32, name=name + "_c", align_bytes=64)
+            s = cod.tile([P, H, T], U8, name=name + "_s", align_bytes=64)
+            return g, c, s
+
+        def quantise(gcs, h):
+            g, c, s = gcs
+            nc.vector.quantize_mx(
+                out=c[:, h, :].bitcast(FP8X4), scales=s[:, h, :], in_=g[:, h, :, :].rearrange("p c t -> p (c t)")
+            )
+
+        def plain_copies(x_sb, gcs, h, name):
+            for ap in range(2):
+                bank = transposes(x_sb, h, ap, name)
+                nc.scalar.copy(
+                    out=gcs[0][:, h, 256 * ap : 256 * (ap + 1), :].bitcast(F32),
+                    in_=bank[:].rearrange("p u c -> p c u"),
+                )
+
+        def query_adds(b, gcs, first_row):
+            for h in range(H):
+                for ap in range(2):
+                    bank = transposes(q_sb[b], h, ap, "q_b")
+                    nc.vector.tensor_tensor(
+                        out=gcs[0][:, h, 256 * ap : 256 * (ap + 1), :].rearrange("p c (u e) -> p c u e", e=2),
+                        in0=bank[:].bitcast(BF16).rearrange("p u (c e) -> p c u e", e=2),
+                        in1=bias4[:, first_row + h, :]
+                        .rearrange("p (u e) -> p u e", e=2)
+                        .unsqueeze(1)
+                        .to_broadcast([P, 256, 2, 2]),
+                        op=ADD,
+                    )
+
+        def mx_pass(lhs, rhs, h, a, name):
+            acc = psum.tile([P, T], F32, name=name, tag="mm")
+            cols = slice(P * a, P * (a + 1))
+            nc.tensor.matmul_mx(
+                out=acc[:],
+                lhsT=lhs[1][:, h, cols].bitcast(FP8X4),
+                lhsT_scale=lhs[2][:, h, cols],
+                rhs=rhs[1][:, h, :].bitcast(FP8X4),
+                rhs_scale=rhs[2][:, h, :],
+                start=True,
+                stop=True,
+            )
+            return acc[:].rearrange("p (al rh) -> p rh al", al=A)
+
+        def park(b, h, qr_op, r_op):
+            z = zt[b * H + h]
+            for a in range(A):
+                nc.scalar.copy(out=z[:, a, 1:PADDED], in_=mx_pass(qr_op, r_op, h, a, "rel"))
+            zf = z[:].rearrange("p a c -> p (a c)")
+            flat = out[b, h].rearrange("t j -> (t j)")
+            row = A * PADDED
+            first = row - T
+            rest = flat[first : T * T].rearrange("(m e) -> m e", e=row)
+            nc.sync.dma_start(out=rest[15 : P - 1, :], in_=zf[16:P, :])
+            nc.sync.dma_start(out=rest[0:15, :], in_=zf[1:16, :])
+            nc.sync.dma_start(out=flat[0:first].rearrange("(o e) -> o e", o=1), in_=zf[0:1, T:row])
+
+        qr = [mx_tiles("qr0"), mx_tiles("qr1")]
+        qw = [mx_tiles("qw0"), mx_tiles("qw1")]
+        kk = [mx_tiles("k0"), mx_tiles("k1")]
+        rr = mx_tiles("r")
+
+        query_adds(0, qr[0], 2)
+        quantise(qr[0], 0)
+        plain_copies(r_sb, rr, 0, "r_b")
+        quantise(qr[0], 1)
+        quantise(rr, 0)
+        plain_copies(r_sb, rr, 1, "r_b")
+        park(0, 0, qr[0], rr)
+        quantise(rr, 1)
+        query_adds(1, qr[1], 2)
+        park(0, 1, qr[0], rr)
+        quantise(qr[1], 0)
+        quantise(qr[1], 1)
+        query_adds(0, qw[0], 0)
+        park(1, 0, qr[1], rr)
+        park(1, 1, qr[1], rr)
+        quantise(qw[0], 0)
+        quantise(qw[0], 1)
+        query_adds(1, qw[1], 0)
+        for h in range(H):
+            plain_copies(k_sb[0], kk[0], h, "k_b")
+        quantise(qw[1], 0)
+        quantise(qw[1], 1)
+        quantise(kk[0], 0)
+        quantise(kk[0], 1)
+        for h in range(H):
+            plain_copies(k_sb[1], kk[1], h, "k_b")
+        quantise(kk[1], 0)
+        quantise(kk[1], 1)
+
+        st = []
+        for b in range(B):
+            for h in range(H):
+                s = big.tile([P, A, T], F32, name="s%d" % (b * H + h), tag="big")
+                nc.sync.dma_start(out=s[:], in_=out[b, h].rearrange("(p a) j -> p a j", a=A))
+                st.append(s)
+        for b in range(B):
+            for h in range(H):
+                s = st[b * H + h]
+                for a in range(A):
+                    nc.vector.tensor_tensor(
+                        out=s[:, a, :], in0=mx_pass(qw[b], kk[b], h, a, "con"), in1=s[:, a, :], op=ADD
+                    )
+                nc.sync.dma_start(out=out[b, h].rearrange("(p a) j -> p a j", a=A), in_=s[:])

@@ -91,19 +91,20 @@ def tile_relativepositionembedding_pa_kernel(tc, q, k, r_w_bias, r_r_bias, rel_p
                     in_=bank[:].rearrange("p u c -> p c u"),
                 )
 
-        def query_adds(b, gcs, first_row):
+        def query_words(b):
+            t = grp.tile([P, H, T, 4], BF16, name="qt%d" % b)
             for h in range(H):
-                for ap in range(2):
-                    bank = transposes(q_sb[b], h, ap, "q_b")
-                    nc.vector.tensor_tensor(
-                        out=gcs[0][:, h, 256 * ap : 256 * (ap + 1), :].rearrange("p c (u e) -> p c u e", e=2),
-                        in0=bank[:].bitcast(BF16).rearrange("p u (c e) -> p c u e", e=2),
-                        in1=bias4[:, first_row + h, :]
-                        .rearrange("p (u e) -> p u e", e=2)
-                        .unsqueeze(1)
-                        .to_broadcast([P, 256, 2, 2]),
-                        op=ADD,
-                    )
+                plain_copies(q_sb[b], (t,), h, "q_b")
+            return t
+
+        def query_adds(qt, gcs, first_row):
+            for h in range(H):
+                nc.vector.tensor_tensor(
+                    out=gcs[0][:, h, :, :],
+                    in0=qt[:, h, :, :],
+                    in1=bias4[:, first_row + h, :].unsqueeze(1).to_broadcast([P, T, 4]),
+                    op=ADD,
+                )
 
         def mx_pass(lhs, rhs, h, a, name):
             acc = psum.tile([P, T], F32, name=name, tag="mm")
@@ -137,24 +138,26 @@ def tile_relativepositionembedding_pa_kernel(tc, q, k, r_w_bias, r_r_bias, rel_p
         kk = [mx_tiles("k0"), mx_tiles("k1")]
         rr = mx_tiles("r")
 
-        query_adds(0, qr[0], 2)
-        quantise(qr[0], 0)
+        qt0 = query_words(0)
+        query_adds(qt0, qr[0], 2)
         plain_copies(r_sb, rr, 0, "r_b")
+        quantise(qr[0], 0)
         quantise(qr[0], 1)
-        quantise(rr, 0)
         plain_copies(r_sb, rr, 1, "r_b")
-        park(0, 0, qr[0], rr)
+        quantise(rr, 0)
         quantise(rr, 1)
-        query_adds(1, qr[1], 2)
+        park(0, 0, qr[0], rr)
+        qt1 = query_words(1)
+        query_adds(qt1, qr[1], 2)
         park(0, 1, qr[0], rr)
         quantise(qr[1], 0)
         quantise(qr[1], 1)
-        query_adds(0, qw[0], 0)
         park(1, 0, qr[1], rr)
+        query_adds(qt0, qw[0], 0)
         park(1, 1, qr[1], rr)
+        query_adds(qt1, qw[1], 0)
         quantise(qw[0], 0)
         quantise(qw[0], 1)
-        query_adds(1, qw[1], 0)
         for h in range(H):
             plain_copies(k_sb[0], kk[0], h, "k_b")
         quantise(qw[1], 0)

@@ -20,7 +20,7 @@ FLOPS = 2 * 2 * B * H * T * T * D
 def tile_relativepositionembedding_pa_kernel(tc, q, k, r_w_bias, r_r_bias, rel_pos_emb, out):
     nc = tc.nc
     with ExitStack() as ctx:
-
+        ctx.enter_context(tc.manual_schedule())
         const = ctx.enter_context(tc.tile_pool(name="const", bufs=1))
         inp = ctx.enter_context(tc.tile_pool(name="inp", bufs=1))
         grp = ctx.enter_context(tc.tile_pool(name="grp", bufs=1))
@@ -91,20 +91,19 @@ def tile_relativepositionembedding_pa_kernel(tc, q, k, r_w_bias, r_r_bias, rel_p
                     in_=bank[:].rearrange("p u c -> p c u"),
                 )
 
-        def query_words(b):
-            t = grp.tile([P, H, T, 4], BF16, name="qt%d" % b)
+        def query_adds(b, gcs, first_row):
             for h in range(H):
-                plain_copies(q_sb[b], (t,), h, "q_b")
-            return t
-
-        def query_adds(qt, gcs, first_row):
-            for h in range(H):
-                nc.vector.tensor_tensor(
-                    out=gcs[0][:, h, :, :],
-                    in0=qt[:, h, :, :],
-                    in1=bias4[:, first_row + h, :].unsqueeze(1).to_broadcast([P, T, 4]),
-                    op=ADD,
-                )
+                for ap in range(2):
+                    bank = transposes(q_sb[b], h, ap, "q_b")
+                    nc.vector.tensor_tensor(
+                        out=gcs[0][:, h, 256 * ap : 256 * (ap + 1), :].rearrange("p c (u e) -> p c u e", e=2),
+                        in0=bank[:].bitcast(BF16).rearrange("p u (c e) -> p c u e", e=2),
+                        in1=bias4[:, first_row + h, :]
+                        .rearrange("p (u e) -> p u e", e=2)
+                        .unsqueeze(1)
+                        .to_broadcast([P, 256, 2, 2]),
+                        op=ADD,
+                    )
 
         def mx_pass(lhs, rhs, h, a, name):
             acc = psum.tile([P, T], F32, name=name, tag="mm")
@@ -138,48 +137,53 @@ def tile_relativepositionembedding_pa_kernel(tc, q, k, r_w_bias, r_r_bias, rel_p
         kk = [mx_tiles("k0"), mx_tiles("k1")]
         rr = mx_tiles("r")
 
-        qt0 = query_words(0)
-        query_adds(qt0, qr[0], 2)
-        plain_copies(r_sb, rr, 0, "r_b")
+        st = [None] * (B * H)
+
+        def reload(i):
+            s = big.tile([P, A, T], F32, name="s%d" % i, tag="big")
+            nc.sync.dma_start(out=s[:], in_=out[i // H, i % H].rearrange("(p a) j -> p a j", a=A))
+            st[i] = s
+
+        def finish(i):
+            b, h = i // H, i % H
+            s = st[i]
+            for a in range(A):
+                nc.vector.tensor_tensor(
+                    out=s[:, a, :], in0=mx_pass(qw[b], kk[b], h, a, "con"), in1=s[:, a, :], op=ADD
+                )
+            nc.scalar.dma_start(out=out[b, h].rearrange("(p a) j -> p a j", a=A), in_=s[:])
+
+        query_adds(0, qr[0], 2)
         quantise(qr[0], 0)
         quantise(qr[0], 1)
-        plain_copies(r_sb, rr, 1, "r_b")
+        for h in range(H):
+            plain_copies(r_sb, rr, h, "r_b")
         quantise(rr, 0)
         quantise(rr, 1)
         park(0, 0, qr[0], rr)
-        qt1 = query_words(1)
-        query_adds(qt1, qr[1], 2)
-        park(0, 1, qr[0], rr)
+        query_adds(1, qr[1], 2)
         quantise(qr[1], 0)
         quantise(qr[1], 1)
-        park(1, 0, qr[1], rr)
-        query_adds(qt0, qw[0], 0)
-        park(1, 1, qr[1], rr)
-        query_adds(qt1, qw[1], 0)
+        park(0, 1, qr[0], rr)
+        reload(0)
+        query_adds(0, qw[0], 0)
         quantise(qw[0], 0)
         quantise(qw[0], 1)
-        for h in range(H):
-            plain_copies(k_sb[0], kk[0], h, "k_b")
+        park(1, 0, qr[1], rr)
+        reload(1)
+        query_adds(1, qw[1], 0)
         quantise(qw[1], 0)
         quantise(qw[1], 1)
+        park(1, 1, qr[1], rr)
+        reload(2)
+        for b in range(B):
+            for h in range(H):
+                plain_copies(k_sb[b], kk[b], h, "k_b")
+        reload(3)
         quantise(kk[0], 0)
         quantise(kk[0], 1)
-        for h in range(H):
-            plain_copies(k_sb[1], kk[1], h, "k_b")
+        finish(0)
         quantise(kk[1], 0)
         quantise(kk[1], 1)
-
-        st = []
-        for b in range(B):
-            for h in range(H):
-                s = big.tile([P, A, T], F32, name="s%d" % (b * H + h), tag="big")
-                nc.sync.dma_start(out=s[:], in_=out[b, h].rearrange("(p a) j -> p a j", a=A))
-                st.append(s)
-        for b in range(B):
-            for h in range(H):
-                s = st[b * H + h]
-                for a in range(A):
-                    nc.vector.tensor_tensor(
-                        out=s[:, a, :], in0=mx_pass(qw[b], kk[b], h, a, "con"), in1=s[:, a, :], op=ADD
-                    )
-                nc.sync.dma_start(out=out[b, h].rearrange("(p a) j -> p a j", a=A), in_=s[:])
+        for i in range(1, B * H):
+            finish(i)

@@ -20,7 +20,7 @@ FLOPS = 2 * 2 * B * H * T * T * D
 def tile_relativepositionembedding_pa_kernel(tc, q, k, r_w_bias, r_r_bias, rel_pos_emb, out):
     nc = tc.nc
     with ExitStack() as ctx:
-        ctx.enter_context(tc.manual_schedule())
+
         const = ctx.enter_context(tc.tile_pool(name="const", bufs=1))
         inp = ctx.enter_context(tc.tile_pool(name="inp", bufs=1))
         grp = ctx.enter_context(tc.tile_pool(name="grp", bufs=1))
@@ -56,18 +56,21 @@ def tile_relativepositionembedding_pa_kernel(tc, q, k, r_w_bias, r_r_bias, rel_p
 
         bias4 = const.tile([P, 4, 4], BF16)
         bw = bias_sb[:].bitcast(F32)
-        bbank = psum.tile([P, 2, 256], F32, name="bbank", tag="tp")
+        bbank = psum.tile([P, 256, 2], F32, name="bbank", tag="tp")
         for u in range(2):
-            nc.tensor.transpose(bbank[:, u, 0:P], bw[:, P * u : P * (u + 1)], ident[:])
-        nc.vector.tensor_copy(out=bias4[:].bitcast(F32), in_=bbank[:, :, 0:4].rearrange("p u r -> p r u"))
+            nc.tensor.transpose(bbank[:, 0:P, u], bw[:, P * u : P * (u + 1)], ident[:])
+        nc.vector.tensor_copy(out=bias4[:].bitcast(F32), in_=bbank[:, 0:4, :])
+        bias_rep = const.tile([P, 4, 256, 4], BF16)
+        for row in (2, 3, 0, 1):
+            nc.scalar.copy(out=bias_rep[:, row, :, :], in_=bias4[:, row, :].unsqueeze(1).to_broadcast([P, 256, 4]))
 
         def transposes(x_sb, h, ap, name):
             xw = x_sb[:].bitcast(F32)
-            bank = psum.tile([P, 2, 256], F32, name=name, tag="tp")
+            bank = psum.tile([P, 256, 2], F32, name=name, tag="tp")
             for u in range(2):
                 for i in range(2):
                     nc.tensor.transpose(
-                        bank[:, u, P * i : P * (i + 1)], xw[:, 2 * ap + i, h, P * u : P * (u + 1)], ident[:]
+                        bank[:, P * i : P * (i + 1), u], xw[:, 2 * ap + i, h, P * u : P * (u + 1)], ident[:]
                     )
             return bank
 
@@ -88,7 +91,7 @@ def tile_relativepositionembedding_pa_kernel(tc, q, k, r_w_bias, r_r_bias, rel_p
                 bank = transposes(x_sb, h, ap, name)
                 nc.scalar.copy(
                     out=gcs[0][:, h, 256 * ap : 256 * (ap + 1), :].bitcast(F32),
-                    in_=bank[:].rearrange("p u c -> p c u"),
+                    in_=bank[:],
                 )
 
         def query_adds(b, gcs, first_row):
@@ -96,12 +99,9 @@ def tile_relativepositionembedding_pa_kernel(tc, q, k, r_w_bias, r_r_bias, rel_p
                 for ap in range(2):
                     bank = transposes(q_sb[b], h, ap, "q_b")
                     nc.vector.tensor_tensor(
-                        out=gcs[0][:, h, 256 * ap : 256 * (ap + 1), :].rearrange("p c (u e) -> p c u e", e=2),
-                        in0=bank[:].bitcast(BF16).rearrange("p u (c e) -> p c u e", e=2),
-                        in1=bias4[:, first_row + h, :]
-                        .rearrange("p (u e) -> p u e", e=2)
-                        .unsqueeze(1)
-                        .to_broadcast([P, 256, 2, 2]),
+                        out=gcs[0][:, h, 256 * ap : 256 * (ap + 1), :],
+                        in0=bank[:].bitcast(BF16),
+                        in1=bias_rep[:, first_row + h, :, :],
                         op=ADD,
                     )
 
@@ -137,53 +137,46 @@ def tile_relativepositionembedding_pa_kernel(tc, q, k, r_w_bias, r_r_bias, rel_p
         kk = [mx_tiles("k0"), mx_tiles("k1")]
         rr = mx_tiles("r")
 
-        st = [None] * (B * H)
-
-        def reload(i):
-            s = big.tile([P, A, T], F32, name="s%d" % i, tag="big")
-            nc.sync.dma_start(out=s[:], in_=out[i // H, i % H].rearrange("(p a) j -> p a j", a=A))
-            st[i] = s
-
-        def finish(i):
-            b, h = i // H, i % H
-            s = st[i]
-            for a in range(A):
-                nc.vector.tensor_tensor(
-                    out=s[:, a, :], in0=mx_pass(qw[b], kk[b], h, a, "con"), in1=s[:, a, :], op=ADD
-                )
-            nc.scalar.dma_start(out=out[b, h].rearrange("(p a) j -> p a j", a=A), in_=s[:])
-
         query_adds(0, qr[0], 2)
         quantise(qr[0], 0)
+        plain_copies(r_sb, rr, 0, "r_b")
         quantise(qr[0], 1)
-        for h in range(H):
-            plain_copies(r_sb, rr, h, "r_b")
         quantise(rr, 0)
-        quantise(rr, 1)
+        plain_copies(r_sb, rr, 1, "r_b")
         park(0, 0, qr[0], rr)
+        quantise(rr, 1)
         query_adds(1, qr[1], 2)
+        park(0, 1, qr[0], rr)
         quantise(qr[1], 0)
         quantise(qr[1], 1)
-        park(0, 1, qr[0], rr)
-        reload(0)
         query_adds(0, qw[0], 0)
+        park(1, 0, qr[1], rr)
+        park(1, 1, qr[1], rr)
         quantise(qw[0], 0)
         quantise(qw[0], 1)
-        park(1, 0, qr[1], rr)
-        reload(1)
         query_adds(1, qw[1], 0)
+        for h in range(H):
+            plain_copies(k_sb[0], kk[0], h, "k_b")
         quantise(qw[1], 0)
         quantise(qw[1], 1)
-        park(1, 1, qr[1], rr)
-        reload(2)
-        for b in range(B):
-            for h in range(H):
-                plain_copies(k_sb[b], kk[b], h, "k_b")
-        reload(3)
         quantise(kk[0], 0)
         quantise(kk[0], 1)
-        finish(0)
+        for h in range(H):
+            plain_copies(k_sb[1], kk[1], h, "k_b")
         quantise(kk[1], 0)
         quantise(kk[1], 1)
-        for i in range(1, B * H):
-            finish(i)
+
+        st = []
+        for b in range(B):
+            for h in range(H):
+                s = big.tile([P, A, T], F32, name="s%d" % (b * H + h), tag="big")
+                nc.sync.dma_start(out=s[:], in_=out[b, h].rearrange("(p a) j -> p a j", a=A))
+                st.append(s)
+        for b in range(B):
+            for h in range(H):
+                s = st[b * H + h]
+                for a in range(A):
+                    nc.vector.tensor_tensor(
+                        out=s[:, a, :], in0=mx_pass(qw[b], kk[b], h, a, "con"), in1=s[:, a, :], op=ADD
+                    )
+                nc.sync.dma_start(out=out[b, h].rearrange("(p a) j -> p a j", a=A), in_=s[:])

@@ -35,18 +35,21 @@ def tile_relativepositionembedding_pa_kernel(tc, q, k, r_w_bias, r_r_bias, rel_p
         ident = const.tile([P, P], F32)
         make_identity(nc, ident[:])
 
-        def load(src, name):
+        def load(src, name, order):
             t = inp.tile([P, A, H, D], BF16, name=name)
-            nc.sync.dma_start(out=t[:], in_=src.rearrange("(p a) h d -> p a h d", a=A))
+            nc.sync.dma_start(out=t[:], in_=src.rearrange(order, a=A))
             return t
+
+        rows_of_out = "(p a) h d -> p a h d"
+        columns_of_out = "(a p) h d -> p a h d"
 
         q_sb = [None, None]
         k_sb = [None, None]
-        q_sb[0] = load(q[0], "q_sb0")
-        r_sb = load(rel_pos_emb, "r_sb")
-        q_sb[1] = load(q[1], "q_sb1")
-        k_sb[0] = load(k[0], "k_sb0")
-        k_sb[1] = load(k[1], "k_sb1")
+        q_sb[0] = load(q[0], "q_sb0", rows_of_out)
+        r_sb = load(rel_pos_emb, "r_sb", columns_of_out)
+        q_sb[1] = load(q[1], "q_sb1", rows_of_out)
+        k_sb[0] = load(k[0], "k_sb0", columns_of_out)
+        k_sb[1] = load(k[1], "k_sb1", columns_of_out)
 
         zt = []
         for i in range(B * H):
@@ -56,21 +59,18 @@ def tile_relativepositionembedding_pa_kernel(tc, q, k, r_w_bias, r_r_bias, rel_p
 
         bias4 = const.tile([P, 4, 4], BF16)
         bw = bias_sb[:].bitcast(F32)
-        bbank = psum.tile([P, 256, 2], F32, name="bbank", tag="tp")
+        bbank = psum.tile([P, 2, 256], F32, name="bbank", tag="tp")
         for u in range(2):
-            nc.tensor.transpose(bbank[:, 0:P, u], bw[:, P * u : P * (u + 1)], ident[:])
-        nc.vector.tensor_copy(out=bias4[:].bitcast(F32), in_=bbank[:, 0:4, :])
-        bias_rep = const.tile([P, 4, 256, 4], BF16)
-        for row in (2, 3, 0, 1):
-            nc.scalar.copy(out=bias_rep[:, row, :, :], in_=bias4[:, row, :].unsqueeze(1).to_broadcast([P, 256, 4]))
+            nc.tensor.transpose(bbank[:, u, 0:P], bw[:, P * u : P * (u + 1)], ident[:])
+        nc.vector.tensor_copy(out=bias4[:].bitcast(F32), in_=bbank[:, :, 0:4].rearrange("p u r -> p r u"))
 
         def transposes(x_sb, h, ap, name):
             xw = x_sb[:].bitcast(F32)
-            bank = psum.tile([P, 256, 2], F32, name=name, tag="tp")
+            bank = psum.tile([P, 2, 256], F32, name=name, tag="tp")
             for u in range(2):
                 for i in range(2):
                     nc.tensor.transpose(
-                        bank[:, P * i : P * (i + 1), u], xw[:, 2 * ap + i, h, P * u : P * (u + 1)], ident[:]
+                        bank[:, u, P * i : P * (i + 1)], xw[:, 2 * ap + i, h, P * u : P * (u + 1)], ident[:]
                     )
             return bank
 
@@ -91,7 +91,7 @@ def tile_relativepositionembedding_pa_kernel(tc, q, k, r_w_bias, r_r_bias, rel_p
                 bank = transposes(x_sb, h, ap, name)
                 nc.scalar.copy(
                     out=gcs[0][:, h, 256 * ap : 256 * (ap + 1), :].bitcast(F32),
-                    in_=bank[:],
+                    in_=bank[:].rearrange("p u c -> p c u"),
                 )
 
         def query_adds(b, gcs, first_row):
@@ -99,9 +99,12 @@ def tile_relativepositionembedding_pa_kernel(tc, q, k, r_w_bias, r_r_bias, rel_p
                 for ap in range(2):
                     bank = transposes(q_sb[b], h, ap, "q_b")
                     nc.vector.tensor_tensor(
-                        out=gcs[0][:, h, 256 * ap : 256 * (ap + 1), :],
-                        in0=bank[:].bitcast(BF16),
-                        in1=bias_rep[:, first_row + h, :, :],
+                        out=gcs[0][:, h, 256 * ap : 256 * (ap + 1), :].rearrange("p c (u e) -> p c u e", e=2),
+                        in0=bank[:].bitcast(BF16).rearrange("p u (c e) -> p c u e", e=2),
+                        in1=bias4[:, first_row + h, :]
+                        .rearrange("p (u e) -> p u e", e=2)
+                        .unsqueeze(1)
+                        .to_broadcast([P, 256, 2, 2]),
                         op=ADD,
                     )
 
@@ -117,7 +120,7 @@ def tile_relativepositionembedding_pa_kernel(tc, q, k, r_w_bias, r_r_bias, rel_p
                 start=True,
                 stop=True,
             )
-            return acc[:].rearrange("p (al rh) -> p rh al", al=A)
+            return acc[:]
 
         def park(b, h, qr_op, r_op):
             z = zt[b * H + h]

@@ -35,21 +35,18 @@ def tile_relativepositionembedding_pa_kernel(tc, q, k, r_w_bias, r_r_bias, rel_p
         ident = const.tile([P, P], F32)
         make_identity(nc, ident[:])
 
-        def load(src, name, order):
+        def load(src, name):
             t = inp.tile([P, A, H, D], BF16, name=name)
-            nc.sync.dma_start(out=t[:], in_=src.rearrange(order, a=A))
+            nc.sync.dma_start(out=t[:], in_=src.rearrange("(p a) h d -> p a h d", a=A))
             return t
-
-        rows_of_out = "(p a) h d -> p a h d"
-        columns_of_out = "(a p) h d -> p a h d"
 
         q_sb = [None, None]
         k_sb = [None, None]
-        q_sb[0] = load(q[0], "q_sb0", rows_of_out)
-        r_sb = load(rel_pos_emb, "r_sb", columns_of_out)
-        q_sb[1] = load(q[1], "q_sb1", rows_of_out)
-        k_sb[0] = load(k[0], "k_sb0", columns_of_out)
-        k_sb[1] = load(k[1], "k_sb1", columns_of_out)
+        q_sb[1] = load(q[1], "q_sb1")
+        r_sb = load(rel_pos_emb, "r_sb")
+        q_sb[0] = load(q[0], "q_sb0")
+        k_sb[1] = load(k[1], "k_sb1")
+        k_sb[0] = load(k[0], "k_sb0")
 
         zt = []
         for i in range(B * H):
@@ -95,7 +92,7 @@ def tile_relativepositionembedding_pa_kernel(tc, q, k, r_w_bias, r_r_bias, rel_p
                 )
 
         def query_adds(b, gcs, first_row):
-            for h in range(H):
+            for h in (1, 0):
                 for ap in range(2):
                     bank = transposes(q_sb[b], h, ap, "q_b")
                     nc.vector.tensor_tensor(
@@ -120,66 +117,68 @@ def tile_relativepositionembedding_pa_kernel(tc, q, k, r_w_bias, r_r_bias, rel_p
                 start=True,
                 stop=True,
             )
-            return acc[:]
+            return acc[:].rearrange("p (al rh) -> p rh al", al=A)
 
         def park(b, h, qr_op, r_op):
             z = zt[b * H + h]
             for a in range(A):
                 nc.scalar.copy(out=z[:, a, 1:PADDED], in_=mx_pass(qr_op, r_op, h, a, "rel"))
             zf = z[:].rearrange("p a c -> p (a c)")
-            flat = out[b, h].rearrange("t j -> (t j)")
             row = A * PADDED
-            first = row - T
-            rest = flat[first : T * T].rearrange("(m e) -> m e", e=row)
-            nc.sync.dma_start(out=rest[15 : P - 1, :], in_=zf[16:P, :])
-            nc.sync.dma_start(out=rest[0:15, :], in_=zf[1:16, :])
-            nc.sync.dma_start(out=flat[0:first].rearrange("(o e) -> o e", o=1), in_=zf[0:1, T:row])
+            base = (b * H + h) * T * T
+            if base > 0:
+                dst = flat_out[base - T : base + T * T].rearrange("(m e) -> m e", e=row)
+                nc.sync.dma_start(out=dst[:, 0:T], in_=zf[:, 0:T])
+                nc.sync.dma_start(out=dst[:, T:row], in_=zf[:, T:row])
+            else:
+                dst = flat_out[0 : P * row].rearrange("(m e) -> m e", e=row)
+                nc.sync.dma_start(out=dst[:, 0 : row - T], in_=zf[:, T:row])
+                for lo, hi in ((64, 128), (32, 64), (16, 32), (1, 16)):
+                    nc.sync.dma_start(out=dst[lo - 1 : hi - 1, row - T : row], in_=zf[lo:hi, 0:T])
 
+        flat_out = out.rearrange("b h t j -> (b h t j)")
         qr = [mx_tiles("qr0"), mx_tiles("qr1")]
         qw = [mx_tiles("qw0"), mx_tiles("qw1")]
         kk = [mx_tiles("k0"), mx_tiles("k1")]
         rr = mx_tiles("r")
 
-        query_adds(0, qr[0], 2)
-        quantise(qr[0], 0)
-        plain_copies(r_sb, rr, 0, "r_b")
-        quantise(qr[0], 1)
-        quantise(rr, 0)
-        plain_copies(r_sb, rr, 1, "r_b")
-        park(0, 0, qr[0], rr)
-        quantise(rr, 1)
         query_adds(1, qr[1], 2)
-        park(0, 1, qr[0], rr)
-        quantise(qr[1], 0)
         quantise(qr[1], 1)
-        query_adds(0, qw[0], 0)
-        park(1, 0, qr[1], rr)
+        plain_copies(r_sb, rr, 1, "r_b")
+        quantise(qr[1], 0)
+        quantise(rr, 1)
+        plain_copies(r_sb, rr, 0, "r_b")
         park(1, 1, qr[1], rr)
-        quantise(qw[0], 0)
-        quantise(qw[0], 1)
+        quantise(rr, 0)
+        query_adds(0, qr[0], 2)
+        park(1, 0, qr[1], rr)
+        quantise(qr[0], 1)
+        quantise(qr[0], 0)
         query_adds(1, qw[1], 0)
-        for h in range(H):
-            plain_copies(k_sb[0], kk[0], h, "k_b")
-        quantise(qw[1], 0)
+        park(0, 1, qr[0], rr)
+        park(0, 0, qr[0], rr)
         quantise(qw[1], 1)
-        quantise(kk[0], 0)
-        quantise(kk[0], 1)
-        for h in range(H):
+        quantise(qw[1], 0)
+        query_adds(0, qw[0], 0)
+        for h in (1, 0):
             plain_copies(k_sb[1], kk[1], h, "k_b")
-        quantise(kk[1], 0)
+        quantise(qw[0], 1)
+        quantise(qw[0], 0)
         quantise(kk[1], 1)
+        quantise(kk[1], 0)
+        for h in (1, 0):
+            plain_copies(k_sb[0], kk[0], h, "k_b")
+        quantise(kk[0], 1)
+        quantise(kk[0], 0)
 
-        st = []
-        for b in range(B):
-            for h in range(H):
-                s = big.tile([P, A, T], F32, name="s%d" % (b * H + h), tag="big")
-                nc.sync.dma_start(out=s[:], in_=out[b, h].rearrange("(p a) j -> p a j", a=A))
-                st.append(s)
-        for b in range(B):
-            for h in range(H):
-                s = st[b * H + h]
-                for a in range(A):
-                    nc.vector.tensor_tensor(
-                        out=s[:, a, :], in0=mx_pass(qw[b], kk[b], h, a, "con"), in1=s[:, a, :], op=ADD
-                    )
-                nc.sync.dma_start(out=out[b, h].rearrange("(p a) j -> p a j", a=A), in_=s[:])
+        st = [None] * (B * H)
+        for i in (3, 2, 1, 0):
+            s = big.tile([P, A, T], F32, name="s%d" % i, tag="big")
+            nc.sync.dma_start(out=s[:], in_=out[i // H, i % H].rearrange("(p a) j -> p a j", a=A))
+            st[i] = s
+        for i in (3, 2, 1, 0):
+            b, h = i // H, i % H
+            s = st[i]
+            for a in range(A):
+                nc.vector.tensor_tensor(out=s[:, a, :], in0=mx_pass(qw[b], kk[b], h, a, "con"), in1=s[:, a, :], op=ADD)
+            nc.sync.dma_start(out=out[b, h].rearrange("(p a) j -> p a j", a=A), in_=s[:])

@@ -133,7 +133,7 @@ def tile_relativepositionembedding_pa_kernel(tc, q, k, r_w_bias, r_r_bias, rel_p
             else:
                 dst = flat_out[0 : P * row].rearrange("(m e) -> m e", e=row)
                 nc.sync.dma_start(out=dst[:, 0 : row - T], in_=zf[:, T:row])
-                for lo, hi in ((64, 128), (32, 64), (16, 32), (1, 16)):
+                for lo, hi in ((64, 128), (32, 64), (16, 32), (8, 16), (4, 8), (2, 4), (1, 2)):
                     nc.sync.dma_start(out=dst[lo - 1 : hi - 1, row - T : row], in_=zf[lo:hi, 0:T])
 
         flat_out = out.rearrange("b h t j -> (b h t j)")

@@ -13,172 +13,163 @@ ADD = mybir.AluOpType.add
 B, T, H, D = 2, 512, 2, 512
 P = 128
 A = T // P
+PACK = 4
 PADDED = T + 1
+RUN = A * PADDED
+BANK_ROWS = 2 * P
 FLOPS = 2 * 2 * B * H * T * T * D
+
+BATCHES = (1, 0)
+HEADS = (1, 0)
 
 
 def tile_relativepositionembedding_pa_kernel(tc, q, k, r_w_bias, r_r_bias, rel_pos_emb, out):
     nc = tc.nc
     with ExitStack() as ctx:
-
         const = ctx.enter_context(tc.tile_pool(name="const", bufs=1))
-        inp = ctx.enter_context(tc.tile_pool(name="inp", bufs=1))
-        grp = ctx.enter_context(tc.tile_pool(name="grp", bufs=1))
-        cod = ctx.enter_context(tc.tile_pool(name="cod", bufs=1))
-        big = ctx.enter_context(tc.tile_pool(name="big", bufs=4))
+        inputs = ctx.enter_context(tc.tile_pool(name="inputs", bufs=1))
+        operands = ctx.enter_context(tc.tile_pool(name="operands", bufs=1))
+        matrices = ctx.enter_context(tc.tile_pool(name="matrices", bufs=B * H))
         psum = ctx.enter_context(tc.psum_pool(name="psum", bufs=4))
 
-        bias_sb = const.tile([P, D], BF16)
-        nc.vector.memset(bias_sb[:], 0.0)
-        nc.sync.dma_start(out=bias_sb[0:2, :], in_=r_w_bias)
-        nc.sync.dma_start(out=bias_sb[2:4, :], in_=r_r_bias)
-        ident = const.tile([P, P], F32)
-        make_identity(nc, ident[:])
+        bias_rows = const.tile([P, D], BF16)
+        nc.vector.memset(bias_rows[:], 0.0)
+        nc.sync.dma_start(out=bias_rows[0:H, :], in_=r_w_bias)
+        nc.sync.dma_start(out=bias_rows[H : 2 * H, :], in_=r_r_bias)
+        identity = const.tile([P, P], F32)
+        make_identity(nc, identity[:])
 
-        def load(src, name):
-            t = inp.tile([P, A, H, D], BF16, name=name)
-            nc.sync.dma_start(out=t[:], in_=src.rearrange("(p a) h d -> p a h d", a=A))
-            return t
+        def load(source, name):
+            tile = inputs.tile([P, A, H, D], BF16, name=name)
+            nc.sync.dma_start(out=tile[:], in_=source.rearrange("(p a) h d -> p a h d", a=A))
+            return tile
 
-        q_sb = [None, None]
-        k_sb = [None, None]
-        q_sb[1] = load(q[1], "q_sb1")
-        r_sb = load(rel_pos_emb, "r_sb")
-        q_sb[0] = load(q[0], "q_sb0")
-        k_sb[1] = load(k[1], "k_sb1")
-        k_sb[0] = load(k[0], "k_sb0")
+        q_in = {BATCHES[0]: load(q[BATCHES[0]], "q_first")}
+        r_in = load(rel_pos_emb, "r_in")
+        q_in[BATCHES[1]] = load(q[BATCHES[1]], "q_second")
+        k_in = {b: load(k[b], "k_in%d" % b) for b in BATCHES}
 
-        zt = []
-        for i in range(B * H):
-            z = big.tile([P, A, PADDED], F32, name="z%d" % i, tag="big")
-            nc.vector.memset(z[:, :, 0:2], 0.0)
-            zt.append(z)
-
-        bias4 = const.tile([P, 4, 4], BF16)
-        bw = bias_sb[:].bitcast(F32)
-        bbank = psum.tile([P, 2, 256], F32, name="bbank", tag="tp")
-        for u in range(2):
-            nc.tensor.transpose(bbank[:, u, 0:P], bw[:, P * u : P * (u + 1)], ident[:])
-        nc.vector.tensor_copy(out=bias4[:].bitcast(F32), in_=bbank[:, :, 0:4].rearrange("p u r -> p r u"))
-
-        def transposes(x_sb, h, ap, name):
-            xw = x_sb[:].bitcast(F32)
-            bank = psum.tile([P, 2, 256], F32, name=name, tag="tp")
+        def transposed_bank(tile, h, half):
+            words = tile[:].bitcast(F32)
+            bank = psum.tile([P, 2, BANK_ROWS], F32, name="transposed", tag="transposed")
             for u in range(2):
                 for i in range(2):
                     nc.tensor.transpose(
-                        bank[:, u, P * i : P * (i + 1)], xw[:, 2 * ap + i, h, P * u : P * (u + 1)], ident[:]
+                        bank[:, u, P * i : P * (i + 1)], words[:, 2 * half + i, h, P * u : P * (u + 1)], identity[:]
                     )
             return bank
 
-        def mx_tiles(name):
-            g = grp.tile([P, H, T, 4], BF16, name=name + "_g", align_bytes=64)
-            c = cod.tile([P, H, T], U32, name=name + "_c", align_bytes=64)
-            s = cod.tile([P, H, T], U8, name=name + "_s", align_bytes=64)
-            return g, c, s
+        def mx_operand(name):
+            values = operands.tile([P, H, T, PACK], BF16, name=name + "_values", align_bytes=64)
+            codes = operands.tile([P, H, T], U32, name=name + "_codes", align_bytes=64)
+            scales = operands.tile([P, H, T], U8, name=name + "_scales", align_bytes=64)
+            return values, codes, scales
 
-        def quantise(gcs, h):
-            g, c, s = gcs
+        def quantise(operand, h):
+            values, codes, scales = operand
             nc.vector.quantize_mx(
-                out=c[:, h, :].bitcast(FP8X4), scales=s[:, h, :], in_=g[:, h, :, :].rearrange("p c t -> p (c t)")
+                out=codes[:, h, :].bitcast(FP8X4),
+                scales=scales[:, h, :],
+                in_=values[:, h, :, :].rearrange("p c t -> p (c t)"),
             )
 
-        def plain_copies(x_sb, gcs, h, name):
-            for ap in range(2):
-                bank = transposes(x_sb, h, ap, name)
-                nc.scalar.copy(
-                    out=gcs[0][:, h, 256 * ap : 256 * (ap + 1), :].bitcast(F32),
-                    in_=bank[:].rearrange("p u c -> p c u"),
-                )
+        def plain_operand(tile, name):
+            operand = mx_operand(name)
+            for h in HEADS:
+                for half in range(2):
+                    bank = transposed_bank(tile, h, half)
+                    nc.scalar.copy(
+                        out=operand[0][:, h, BANK_ROWS * half : BANK_ROWS * (half + 1), :].bitcast(F32),
+                        in_=bank[:].rearrange("p u c -> p c u"),
+                    )
+                quantise(operand, h)
+            return operand
 
-        def query_adds(b, gcs, first_row):
-            for h in (1, 0):
-                for ap in range(2):
-                    bank = transposes(q_sb[b], h, ap, "q_b")
+        def query_operand(b, first_bias_row, name):
+            operand = mx_operand(name)
+            for h in HEADS:
+                for half in range(2):
+                    bank = transposed_bank(q_in[b], h, half)
                     nc.vector.tensor_tensor(
-                        out=gcs[0][:, h, 256 * ap : 256 * (ap + 1), :].rearrange("p c (u e) -> p c u e", e=2),
+                        out=operand[0][:, h, BANK_ROWS * half : BANK_ROWS * (half + 1), :].rearrange(
+                            "p c (u e) -> p c u e", e=2
+                        ),
                         in0=bank[:].bitcast(BF16).rearrange("p u (c e) -> p c u e", e=2),
-                        in1=bias4[:, first_row + h, :]
+                        in1=bias[:, first_bias_row + h, :]
                         .rearrange("p (u e) -> p u e", e=2)
                         .unsqueeze(1)
-                        .to_broadcast([P, 256, 2, 2]),
+                        .to_broadcast([P, BANK_ROWS, 2, 2]),
                         op=ADD,
                     )
+            for h in HEADS:
+                quantise(operand, h)
+            return operand
 
-        def mx_pass(lhs, rhs, h, a, name):
-            acc = psum.tile([P, T], F32, name=name, tag="mm")
-            cols = slice(P * a, P * (a + 1))
+        def product(queries, others, h, a):
+            bank = psum.tile([P, T], F32, name="product", tag="product")
+            block = slice(P * a, P * (a + 1))
             nc.tensor.matmul_mx(
-                out=acc[:],
-                lhsT=lhs[1][:, h, cols].bitcast(FP8X4),
-                lhsT_scale=lhs[2][:, h, cols],
-                rhs=rhs[1][:, h, :].bitcast(FP8X4),
-                rhs_scale=rhs[2][:, h, :],
+                out=bank[:],
+                lhsT=queries[1][:, h, block].bitcast(FP8X4),
+                lhsT_scale=queries[2][:, h, block],
+                rhs=others[1][:, h, :].bitcast(FP8X4),
+                rhs_scale=others[2][:, h, :],
                 start=True,
                 stop=True,
             )
-            return acc[:].rearrange("p (al rh) -> p rh al", al=A)
-
-        def park(b, h, qr_op, r_op):
-            z = zt[b * H + h]
-            for a in range(A):
-                nc.scalar.copy(out=z[:, a, 1:PADDED], in_=mx_pass(qr_op, r_op, h, a, "rel"))
-            zf = z[:].rearrange("p a c -> p (a c)")
-            row = A * PADDED
-            base = (b * H + h) * T * T
-            if base > 0:
-                dst = flat_out[base - T : base + T * T].rearrange("(m e) -> m e", e=row)
-                nc.sync.dma_start(out=dst[:, 0:T], in_=zf[:, 0:T])
-                nc.sync.dma_start(out=dst[:, T:row], in_=zf[:, T:row])
-            else:
-                dst = flat_out[0 : P * row].rearrange("(m e) -> m e", e=row)
-                nc.sync.dma_start(out=dst[:, 0 : row - T], in_=zf[:, T:row])
-                for lo, hi in ((64, 128), (32, 64), (16, 32), (8, 16), (4, 8), (2, 4), (1, 2)):
-                    nc.sync.dma_start(out=dst[lo - 1 : hi - 1, row - T : row], in_=zf[lo:hi, 0:T])
+            return bank[:].rearrange("p (a r) -> p r a", a=A)
 
         flat_out = out.rearrange("b h t j -> (b h t j)")
-        qr = [mx_tiles("qr0"), mx_tiles("qr1")]
-        qw = [mx_tiles("qw0"), mx_tiles("qw1")]
-        kk = [mx_tiles("k0"), mx_tiles("k1")]
-        rr = mx_tiles("r")
 
-        query_adds(1, qr[1], 2)
-        quantise(qr[1], 1)
-        plain_copies(r_sb, rr, 1, "r_b")
-        quantise(qr[1], 0)
-        quantise(rr, 1)
-        plain_copies(r_sb, rr, 0, "r_b")
-        park(1, 1, qr[1], rr)
-        quantise(rr, 0)
-        query_adds(0, qr[0], 2)
-        park(1, 0, qr[1], rr)
-        quantise(qr[0], 1)
-        quantise(qr[0], 0)
-        query_adds(1, qw[1], 0)
-        park(0, 1, qr[0], rr)
-        park(0, 0, qr[0], rr)
-        quantise(qw[1], 1)
-        quantise(qw[1], 0)
-        query_adds(0, qw[0], 0)
-        for h in (1, 0):
-            plain_copies(k_sb[1], kk[1], h, "k_b")
-        quantise(qw[0], 1)
-        quantise(qw[0], 0)
-        quantise(kk[1], 1)
-        quantise(kk[1], 0)
-        for h in (1, 0):
-            plain_copies(k_sb[0], kk[0], h, "k_b")
-        quantise(kk[0], 1)
-        quantise(kk[0], 0)
-
-        st = [None] * (B * H)
-        for i in (3, 2, 1, 0):
-            s = big.tile([P, A, T], F32, name="s%d" % i, tag="big")
-            nc.sync.dma_start(out=s[:], in_=out[i // H, i % H].rearrange("(p a) j -> p a j", a=A))
-            st[i] = s
-        for i in (3, 2, 1, 0):
-            b, h = i // H, i % H
-            s = st[i]
+        def park(b, h):
+            pad = padded[b * H + h]
             for a in range(A):
-                nc.vector.tensor_tensor(out=s[:, a, :], in0=mx_pass(qw[b], kk[b], h, a, "con"), in1=s[:, a, :], op=ADD)
-            nc.sync.dma_start(out=out[b, h].rearrange("(p a) j -> p a j", a=A), in_=s[:])
+                nc.scalar.copy(out=pad[:, a, 1:PADDED], in_=product(q_rel[b], r_op, h, a))
+            flat_pad = pad[:].rearrange("p a c -> p (a c)")
+            start = (b * H + h) * T * T
+            if start > 0:
+                place = flat_out[start - T : start + T * T].rearrange("(p e) -> p e", e=RUN)
+                nc.sync.dma_start(out=place[:, 0:T], in_=flat_pad[:, 0:T])
+                nc.sync.dma_start(out=place[:, T:RUN], in_=flat_pad[:, T:RUN])
+            else:
+                place = flat_out[0 : P * RUN].rearrange("(p e) -> p e", e=RUN)
+                nc.sync.dma_start(out=place[:, 0 : RUN - T], in_=flat_pad[:, T:RUN])
+                for low, high in ((64, 128), (32, 64), (16, 32), (1, 16)):
+                    nc.sync.dma_start(out=place[low - 1 : high - 1, RUN - T : RUN], in_=flat_pad[low:high, 0:T])
+
+        padded = []
+        for m in range(B * H):
+            pad = matrices.tile([P, A, PADDED], F32, name="padded%d" % m, tag="matrix")
+            nc.vector.memset(pad[:, :, 0:2], 0.0)
+            padded.append(pad)
+
+        bias = const.tile([P, 2 * H, PACK], BF16)
+        bias_bank = psum.tile([P, 2, BANK_ROWS], F32, name="bias_bank", tag="transposed")
+        for u in range(2):
+            nc.tensor.transpose(bias_bank[:, u, 0:P], bias_rows[:].bitcast(F32)[:, P * u : P * (u + 1)], identity[:])
+        nc.vector.tensor_copy(out=bias[:].bitcast(F32), in_=bias_bank[:, :, 0 : 2 * H].rearrange("p u r -> p r u"))
+
+        q_rel = {}
+        for b in BATCHES:
+            q_rel[b] = query_operand(b, H, "q_rel%d" % b)
+            if b == BATCHES[0]:
+                r_op = plain_operand(r_in, "r")
+            for h in HEADS:
+                park(b, h)
+
+        q_content = {b: query_operand(b, 0, "q_content%d" % b) for b in BATCHES}
+        k_op = {b: plain_operand(k_in[b], "k%d" % b) for b in BATCHES}
+
+        shifted = {}
+        for b in BATCHES:
+            for h in HEADS:
+                shifted[(b, h)] = matrices.tile([P, A, T], F32, name="shifted%d" % (b * H + h), tag="matrix")
+                nc.sync.dma_start(out=shifted[(b, h)][:], in_=out[b, h].rearrange("(p a) j -> p a j", a=A))
+        for b in BATCHES:
+            for h in HEADS:
+                sums = shifted[(b, h)]
+                for a in range(A):
+                    nc.vector.tensor_tensor(
+                        out=sums[:, a, :], in0=product(q_content[b], k_op[b], h, a), in1=sums[:, a, :], op=ADD
+                    )
+                nc.sync.dma_start(out=out[b, h].rearrange("(p a) j -> p a j", a=A), in_=sums[:])

from contextlib import ExitStack

import concourse.mybir as mybir
from concourse.masks import make_identity

F32 = mybir.dt.float32
BF16 = mybir.dt.bfloat16
U32 = mybir.dt.uint32
U8 = mybir.dt.uint8
FP8X4 = mybir.dt.float8_e4m3fn_x4
ADD = mybir.AluOpType.add

B, T, H, D = 2, 512, 2, 512
P = 128
A = T // P
PACK = 4
PADDED = T + 1
RUN = A * PADDED
BANK_ROWS = 2 * P
FLOPS = 2 * 2 * B * H * T * T * D

BATCHES = (1, 0)
HEADS = (1, 0)


def tile_relativepositionembedding_pa_kernel(tc, q, k, r_w_bias, r_r_bias, rel_pos_emb, out):
    nc = tc.nc
    with ExitStack() as ctx:
        const = ctx.enter_context(tc.tile_pool(name="const", bufs=1))
        inputs = ctx.enter_context(tc.tile_pool(name="inputs", bufs=1))
        operands = ctx.enter_context(tc.tile_pool(name="operands", bufs=1))
        matrices = ctx.enter_context(tc.tile_pool(name="matrices", bufs=B * H))
        psum = ctx.enter_context(tc.psum_pool(name="psum", bufs=4))

        bias_rows = const.tile([P, D], BF16)
        nc.vector.memset(bias_rows[:], 0.0)
        nc.sync.dma_start(out=bias_rows[0:H, :], in_=r_w_bias)
        nc.sync.dma_start(out=bias_rows[H : 2 * H, :], in_=r_r_bias)
        identity = const.tile([P, P], F32)
        make_identity(nc, identity[:])

        def load(source, name):
            tile = inputs.tile([P, A, H, D], BF16, name=name)
            nc.sync.dma_start(out=tile[:], in_=source.rearrange("(p a) h d -> p a h d", a=A))
            return tile

        q_in = {BATCHES[0]: load(q[BATCHES[0]], "q_first")}
        r_in = load(rel_pos_emb, "r_in")
        q_in[BATCHES[1]] = load(q[BATCHES[1]], "q_second")
        k_in = {b: load(k[b], "k_in%d" % b) for b in BATCHES}

        def transposed_bank(tile, h, half):
            words = tile[:].bitcast(F32)
            bank = psum.tile([P, 2, BANK_ROWS], F32, name="transposed", tag="transposed")
            for u in range(2):
                for i in range(2):
                    nc.tensor.transpose(
                        bank[:, u, P * i : P * (i + 1)], words[:, 2 * half + i, h, P * u : P * (u + 1)], identity[:]
                    )
            return bank

        def mx_operand(name):
            values = operands.tile([P, H, T, PACK], BF16, name=name + "_values", align_bytes=64)
            codes = operands.tile([P, H, T], U32, name=name + "_codes", align_bytes=64)
            scales = operands.tile([P, H, T], U8, name=name + "_scales", align_bytes=64)
            return values, codes, scales

        def quantise(operand, h):
            values, codes, scales = operand
            nc.vector.quantize_mx(
                out=codes[:, h, :].bitcast(FP8X4),
                scales=scales[:, h, :],
                in_=values[:, h, :, :].rearrange("p c t -> p (c t)"),
            )

        def plain_operand(tile, name):
            operand = mx_operand(name)
            for h in HEADS:
                for half in range(2):
                    bank = transposed_bank(tile, h, half)
                    nc.scalar.copy(
                        out=operand[0][:, h, BANK_ROWS * half : BANK_ROWS * (half + 1), :].bitcast(F32),
                        in_=bank[:].rearrange("p u c -> p c u"),
                    )
                quantise(operand, h)
            return operand

        def query_operand(b, first_bias_row, name):
            operand = mx_operand(name)
            for h in HEADS:
                for half in range(2):
                    bank = transposed_bank(q_in[b], h, half)
                    nc.vector.tensor_tensor(
                        out=operand[0][:, h, BANK_ROWS * half : BANK_ROWS * (half + 1), :].rearrange(
                            "p c (u e) -> p c u e", e=2
                        ),
                        in0=bank[:].bitcast(BF16).rearrange("p u (c e) -> p c u e", e=2),
                        in1=bias[:, first_bias_row + h, :]
                        .rearrange("p (u e) -> p u e", e=2)
                        .unsqueeze(1)
                        .to_broadcast([P, BANK_ROWS, 2, 2]),
                        op=ADD,
                    )
            for h in HEADS:
                quantise(operand, h)
            return operand

        def product(queries, others, h, a):
            bank = psum.tile([P, T], F32, name="product", tag="product")
            block = slice(P * a, P * (a + 1))
            nc.tensor.matmul_mx(
                out=bank[:],
                lhsT=queries[1][:, h, block].bitcast(FP8X4),
                lhsT_scale=queries[2][:, h, block],
                rhs=others[1][:, h, :].bitcast(FP8X4),
                rhs_scale=others[2][:, h, :],
                start=True,
                stop=True,
            )
            return bank[:].rearrange("p (a r) -> p r a", a=A)

        flat_out = out.rearrange("b h t j -> (b h t j)")

        def park(b, h):
            pad = padded[b * H + h]
            for a in range(A):
                nc.scalar.copy(out=pad[:, a, 1:PADDED], in_=product(q_rel[b], r_op, h, a))
            flat_pad = pad[:].rearrange("p a c -> p (a c)")
            start = (b * H + h) * T * T
            if start > 0:
                place = flat_out[start - T : start + T * T].rearrange("(p e) -> p e", e=RUN)
                nc.sync.dma_start(out=place[:, 0:T], in_=flat_pad[:, 0:T])
                nc.sync.dma_start(out=place[:, T:RUN], in_=flat_pad[:, T:RUN])
            else:
                place = flat_out[0 : P * RUN].rearrange("(p e) -> p e", e=RUN)
                nc.sync.dma_start(out=place[:, 0 : RUN - T], in_=flat_pad[:, T:RUN])
                for low, high in ((64, 128), (32, 64), (16, 32), (1, 16)):
                    nc.sync.dma_start(out=place[low - 1 : high - 1, RUN - T : RUN], in_=flat_pad[low:high, 0:T])

        padded = []
        for m in range(B * H):
            pad = matrices.tile([P, A, PADDED], F32, name="padded%d" % m, tag="matrix")
            nc.vector.memset(pad[:, :, 0:2], 0.0)
            padded.append(pad)

        bias = const.tile([P, 2 * H, PACK], BF16)
        bias_bank = psum.tile([P, 2, BANK_ROWS], F32, name="bias_bank", tag="transposed")
        for u in range(2):
            nc.tensor.transpose(bias_bank[:, u, 0:P], bias_rows[:].bitcast(F32)[:, P * u : P * (u + 1)], identity[:])
        nc.vector.tensor_copy(out=bias[:].bitcast(F32), in_=bias_bank[:, :, 0 : 2 * H].rearrange("p u r -> p r u"))

        q_rel = {}
        for b in BATCHES:
            q_rel[b] = query_operand(b, H, "q_rel%d" % b)
            if b == BATCHES[0]:
                r_op = plain_operand(r_in, "r")
            for h in HEADS:
                park(b, h)

        q_content = {b: query_operand(b, 0, "q_content%d" % b) for b in BATCHES}
        k_op = {b: plain_operand(k_in[b], "k%d" % b) for b in BATCHES}

        shifted = {}
        for b in BATCHES:
            for h in HEADS:
                shifted[(b, h)] = matrices.tile([P, A, T], F32, name="shifted%d" % (b * H + h), tag="matrix")
                nc.sync.dma_start(out=shifted[(b, h)][:], in_=out[b, h].rearrange("(p a) j -> p a j", a=A))
        for b in BATCHES:
            for h in HEADS:
                sums = shifted[(b, h)]
                for a in range(A):
                    nc.vector.tensor_tensor(
                        out=sums[:, a, :], in0=product(q_content[b], k_op[b], h, a), in1=sums[:, a, :], op=ADD
                    )
                nc.sync.dma_start(out=out[b, h].rearrange("(p a) j -> p a j", a=A), in_=sums[:])
